import numpy as np
import ml_dtypes

BF16 = ml_dtypes.bfloat16


def bf(x):
    return np.asarray(x, np.float32).astype(BF16)


def f32(x):
    return np.asarray(x, np.float32)


def f64(x):
    return np.asarray(x).astype(np.float64)


def striped(idx):
    return np.tile(idx.reshape(-1, 16).T, (8, 1))


D, S, H, E, L, B, N = 128, 2048, 256, 128, 4, 512, 2048
ERF_LIM, ERF_TERMS = 6.0, 150


def erf(a):
    a = np.asarray(a, np.float64)
    c = np.clip(a, -ERF_LIM, ERF_LIM)
    term = c.copy()
    total = c.copy()
    for n in range(1, ERF_TERMS):
        term = term * 2.0 * c * c / (2.0 * n + 1.0)
        total = total + term
    r = 2.0 / np.sqrt(np.pi) * np.exp(-c * c) * total
    return np.where(np.abs(a) > ERF_LIM, np.sign(a), r)


def gelu_erf(v):
    return 0.5 * v * (1.0 + erf(v / np.sqrt(2.0)))


def setup_inputs():
    return {"table": bf(np.random.standard_normal((D, S))), "w1": bf(np.random.standard_normal((D, H)) * np.sqrt(L / D)), "b1": f32(0.1 * np.random.standard_normal((H, 1))), "w2": bf(np.random.standard_normal((H, E)) * 2.0 / np.sqrt(H)), "b2": f32(0.1 * np.random.standard_normal((E, 1))), "offs": striped(np.random.permutation(np.tile(np.arange(S), 2))[:N])}


def reference(table, w1, b1, w2, b2, offs):
    idx = offs[:16].T.reshape(-1)
    proj = f64(w1).T @ f64(table)[:, idx]
    u = proj.reshape(H, B, L).sum(axis=2) / L + f64(b1)
    a = gelu_erf(u)
    z = f64(w2).T @ a + f64(b2)
    p = np.exp(z - z.max(axis=0, keepdims=True))
    return p / p.sum(axis=0, keepdims=True)

@@ -1,0 +1,98 @@
+import concourse.mybir as mybir
+from concourse.masks import make_identity
+
+P = 128
+WORDS = 2048
+HIDDEN = 256
+TOKENS = 4
+LIST = 2048
+PIECE = 512
+SEQS = PIECE // TOKENS
+N_PIECES = LIST // PIECE
+N_HALVES = HIDDEN // P
+PIECE_COLS = PIECE // 16
+
+FLOPS = 2 * P * HIDDEN * LIST + 2 * HIDDEN * P * (LIST // TOKENS)
+
+BF16, F32, U16 = mybir.dt.bfloat16, mybir.dt.float32, mybir.dt.uint16
+ACT = mybir.ActivationFunctionType
+ALU = mybir.AluOpType
+X = mybir.AxisListType.X
+
+
+def tile_heterogeneousgatingnetwork_kernel(tc, table, w1, b1, w2, b2, offs, out):
+    nc = tc.nc
+    with (
+        tc.tile_pool(name="held", bufs=1) as held,
+        tc.tile_pool(name="hidden", bufs=N_PIECES * N_HALVES) as hidden,
+        tc.tile_pool(name="work", bufs=3) as work,
+    ):
+        offsets = held.tile([P, LIST // 16], U16, name="offsets")
+        nc.sync.dma_start(offsets[:], offs)
+        w1_sb = held.tile([P, HIDDEN], BF16, name="w1_sb")
+        nc.scalar.dma_start(w1_sb[:], w1)
+        table_sb = held.tile([P, WORDS], BF16, name="table_sb")
+        quarter = WORDS // 4
+        for q in range(4):
+            queue = nc.sync if q % 2 == 0 else nc.scalar
+            queue.dma_start(
+                table_sb[:, q * quarter : (q + 1) * quarter], table[:, q * quarter : (q + 1) * quarter]
+            )
+        w2_sb = held.tile([P, N_HALVES, P], BF16, name="w2_sb")
+        nc.scalar.dma_start(w2_sb[:], w2.rearrange("(h i) e -> i h e", i=P))
+        b1_half = [held.tile([P, 1], F32, name=f"b1_half{h}") for h in range(N_HALVES)]
+        for h in range(N_HALVES):
+            nc.sync.dma_start(b1_half[h][:], b1[h * P : (h + 1) * P, :])
+        b2_rows = held.tile([P, P], F32, name="b2_rows")
+        nc.sync.dma_start(b2_rows[:], b2.rearrange("e o -> (e o)").partition_broadcast(P))
+        identity = held.tile([P, P], F32, name="identity")
+        make_identity(nc, identity[:])
+
+        a = [[None] * N_HALVES for piece in range(N_PIECES)]
+        with tc.psum_pool(name="proj_banks", bufs=N_PIECES * N_HALVES) as proj_banks:
+            for piece in range(N_PIECES):
+                piece_offsets = offsets[:, piece * PIECE_COLS : (piece + 1) * PIECE_COLS]
+                for h in range(N_HALVES):
+                    proj = proj_banks.tile([P, PIECE], F32, name="proj")
+                    nc.tensor.matmul(
+                        proj[:],
+                        w1_sb[:, h * P : (h + 1) * P],
+                        table_sb[:].indirect(piece_offsets),
+                        start=True,
+                        stop=True,
+                    )
+                    token_sum = work.tile([P, SEQS], F32, name="token_sum")
+                    nc.vector.tensor_reduce(
+                        token_sum[:], proj[:].rearrange("i (r t) -> i r t", t=TOKENS), axis=X, op=ALU.add
+                    )
+                    a[piece][h] = hidden.tile([P, SEQS], BF16, name="a")
+                    nc.scalar.activation(
+                        a[piece][h][:], token_sum[:], ACT.Gelu, bias=b1_half[h][:], scale=1.0 / TOKENS
+                    )
+
+        with (
+            tc.psum_pool(name="gate_banks", bufs=N_PIECES) as gate_banks,
+            tc.psum_pool(name="flip_banks", bufs=N_PIECES) as flip_banks,
+        ):
+            for piece in range(N_PIECES):
+                z_bank = gate_banks.tile([P, P], F32, name="z_bank")
+                for h in range(N_HALVES):
+                    nc.tensor.matmul(
+                        z_bank[:], a[piece][h][:], w2_sb[:, h, :], start=(h == 0), stop=(h == N_HALVES - 1)
+                    )
+                z = work.tile([P, P], F32, name="z")
+                nc.vector.tensor_tensor(z[:], z_bank[:], b2_rows[:], ALU.add)
+                minus_max = work.tile([P, 1], F32, name="minus_max")
+                nc.vector.tensor_reduce(minus_max[:], z[:], axis=X, op=ALU.max, negate=True)
+                e = work.tile([P, P], F32, name="e")
+                e_sum = work.tile([P, 1], F32, name="e_sum")
+                nc.scalar.activation(e[:], z[:], ACT.Exp, bias=minus_max[:], accum_out=e_sum[:])
+                inverse_sum = work.tile([P, 1], F32, name="inverse_sum")
+                nc.vector.reciprocal(inverse_sum[:], e_sum[:])
+                share = work.tile([P, P], F32, name="share")
+                nc.vector.tensor_scalar_mul(share[:], e[:], inverse_sum[:])
+                flipped = flip_banks.tile([P, P], F32, name="flipped")
+                nc.tensor.transpose(flipped[:], share[:], identity[:])
+                out_block = work.tile([P, SEQS], F32, name="out_block")
+                nc.scalar.copy(out_block[:], flipped[:])
+                nc.sync.dma_start(out[:, piece * SEQS : (piece + 1) * SEQS], out_block[:])

@@ -11,6 +11,7 @@ SEQS = PIECE // TOKENS
 N_PIECES = LIST // PIECE
 N_HALVES = HIDDEN // P
 PIECE_COLS = PIECE // 16
+WARM_MATMULS = 6
 
 FLOPS = 2 * P * HIDDEN * LIST + 2 * HIDDEN * P * (LIST // TOKENS)
 
@@ -47,6 +48,13 @@ def tile_heterogeneousgatingnetwork_kernel(tc, table, w1, b1, w2, b2, offs, out)
         nc.sync.dma_start(b2_rows[:], b2.rearrange("e o -> (e o)").partition_broadcast(P))
         identity = held.tile([P, P], F32, name="identity")
         make_identity(nc, identity[:])
+
+        zeros = held.tile([P, PIECE], BF16, name="zeros")
+        nc.vector.memset(zeros[:], 0.0)
+        with tc.psum_pool(name="warm_banks", bufs=1) as warm_banks:
+            warm = warm_banks.tile([P, PIECE], F32, name="warm")
+            for i in range(WARM_MATMULS):
+                nc.tensor.matmul(warm[:], zeros[:, :P], zeros[:], start=True, stop=True)
 
         a = [[None] * N_HALVES for piece in range(N_PIECES)]
         with tc.psum_pool(name="proj_banks", bufs=N_PIECES * N_HALVES) as proj_banks:

@@ -11,7 +11,6 @@ SEQS = PIECE // TOKENS
 N_PIECES = LIST // PIECE
 N_HALVES = HIDDEN // P
 PIECE_COLS = PIECE // 16
-WARM_MATMULS = 6
 
 FLOPS = 2 * P * HIDDEN * LIST + 2 * HIDDEN * P * (LIST // TOKENS)
 
@@ -27,6 +26,7 @@ def tile_heterogeneousgatingnetwork_kernel(tc, table, w1, b1, w2, b2, offs, out)
         tc.tile_pool(name="held", bufs=1) as held,
         tc.tile_pool(name="hidden", bufs=N_PIECES * N_HALVES) as hidden,
         tc.tile_pool(name="work", bufs=3) as work,
+        tc.tile_pool(name="blocks", bufs=N_PIECES) as blocks,
     ):
         offsets = held.tile([P, LIST // 16], U16, name="offsets")
         nc.sync.dma_start(offsets[:], offs)
@@ -48,13 +48,6 @@ def tile_heterogeneousgatingnetwork_kernel(tc, table, w1, b1, w2, b2, offs, out)
         nc.sync.dma_start(b2_rows[:], b2.rearrange("e o -> (e o)").partition_broadcast(P))
         identity = held.tile([P, P], F32, name="identity")
         make_identity(nc, identity[:])
-
-        zeros = held.tile([P, PIECE], BF16, name="zeros")
-        nc.vector.memset(zeros[:], 0.0)
-        with tc.psum_pool(name="warm_banks", bufs=1) as warm_banks:
-            warm = warm_banks.tile([P, PIECE], F32, name="warm")
-            for i in range(WARM_MATMULS):
-                nc.tensor.matmul(warm[:], zeros[:, :P], zeros[:], start=True, stop=True)
 
         a = [[None] * N_HALVES for piece in range(N_PIECES)]
         with tc.psum_pool(name="proj_banks", bufs=N_PIECES * N_HALVES) as proj_banks:
@@ -82,25 +75,31 @@ def tile_heterogeneousgatingnetwork_kernel(tc, table, w1, b1, w2, b2, offs, out)
             tc.psum_pool(name="gate_banks", bufs=N_PIECES) as gate_banks,
             tc.psum_pool(name="flip_banks", bufs=N_PIECES) as flip_banks,
         ):
+            z, minus_max = [], []
             for piece in range(N_PIECES):
                 z_bank = gate_banks.tile([P, P], F32, name="z_bank")
                 for h in range(N_HALVES):
                     nc.tensor.matmul(
                         z_bank[:], a[piece][h][:], w2_sb[:, h, :], start=(h == 0), stop=(h == N_HALVES - 1)
                     )
-                z = work.tile([P, P], F32, name="z")
-                nc.vector.tensor_tensor(z[:], z_bank[:], b2_rows[:], ALU.add)
-                minus_max = work.tile([P, 1], F32, name="minus_max")
-                nc.vector.tensor_reduce(minus_max[:], z[:], axis=X, op=ALU.max, negate=True)
-                e = work.tile([P, P], F32, name="e")
-                e_sum = work.tile([P, 1], F32, name="e_sum")
-                nc.scalar.activation(e[:], z[:], ACT.Exp, bias=minus_max[:], accum_out=e_sum[:])
-                inverse_sum = work.tile([P, 1], F32, name="inverse_sum")
-                nc.vector.reciprocal(inverse_sum[:], e_sum[:])
-                share = work.tile([P, P], F32, name="share")
-                nc.vector.tensor_scalar_mul(share[:], e[:], inverse_sum[:])
+                z.append(blocks.tile([P, P], F32, name="z"))
+                nc.vector.tensor_tensor(z[piece][:], z_bank[:], b2_rows[:], ALU.add)
+                minus_max.append(blocks.tile([P, 1], F32, name="minus_max"))
+                nc.vector.tensor_reduce(minus_max[piece][:], z[piece][:], axis=X, op=ALU.max, negate=True)
+            e, e_sum = [], []
+            for piece in range(N_PIECES):
+                e.append(blocks.tile([P, P], F32, name="e"))
+                e_sum.append(blocks.tile([P, 1], F32, name="e_sum"))
+                nc.scalar.activation(
+                    e[piece][:], z[piece][:], ACT.Exp, bias=minus_max[piece][:], accum_out=e_sum[piece][:]
+                )
+            for piece in range(N_PIECES):
+                inverse_sum = blocks.tile([P, 1], F32, name="inverse_sum")
+                nc.vector.reciprocal(inverse_sum[:], e_sum[piece][:])
+                share = blocks.tile([P, P], F32, name="share")
+                nc.vector.tensor_scalar_mul(share[:], e[piece][:], inverse_sum[:])
                 flipped = flip_banks.tile([P, P], F32, name="flipped")
                 nc.tensor.transpose(flipped[:], share[:], identity[:])
-                out_block = work.tile([P, SEQS], F32, name="out_block")
+                out_block = blocks.tile([P, SEQS], F32, name="out_block")
                 nc.scalar.copy(out_block[:], flipped[:])
                 nc.sync.dma_start(out[:, piece * SEQS : (piece + 1) * SEQS], out_block[:])

@@ -75,23 +75,22 @@ def tile_heterogeneousgatingnetwork_kernel(tc, table, w1, b1, w2, b2, offs, out)
             tc.psum_pool(name="gate_banks", bufs=N_PIECES) as gate_banks,
             tc.psum_pool(name="flip_banks", bufs=N_PIECES) as flip_banks,
         ):
-            z, minus_max = [], []
+            z_bank, minus_max = [], []
             for piece in range(N_PIECES):
-                z_bank = gate_banks.tile([P, P], F32, name="z_bank")
+                z_bank.append(gate_banks.tile([P, P], F32, name="z_bank"))
+                nc.tensor.matmul(z_bank[piece][:], identity[:], b2_rows[:], start=True, stop=False)
                 for h in range(N_HALVES):
                     nc.tensor.matmul(
-                        z_bank[:], a[piece][h][:], w2_sb[:, h, :], start=(h == 0), stop=(h == N_HALVES - 1)
+                        z_bank[piece][:], a[piece][h][:], w2_sb[:, h, :], start=False, stop=(h == N_HALVES - 1)
                     )
-                z.append(blocks.tile([P, P], F32, name="z"))
-                nc.vector.tensor_tensor(z[piece][:], z_bank[:], b2_rows[:], ALU.add)
                 minus_max.append(blocks.tile([P, 1], F32, name="minus_max"))
-                nc.vector.tensor_reduce(minus_max[piece][:], z[piece][:], axis=X, op=ALU.max, negate=True)
+                nc.vector.tensor_reduce(minus_max[piece][:], z_bank[piece][:], axis=X, op=ALU.max, negate=True)
             e, e_sum = [], []
             for piece in range(N_PIECES):
                 e.append(blocks.tile([P, P], F32, name="e"))
                 e_sum.append(blocks.tile([P, 1], F32, name="e_sum"))
                 nc.scalar.activation(
-                    e[piece][:], z[piece][:], ACT.Exp, bias=minus_max[piece][:], accum_out=e_sum[piece][:]
+                    e[piece][:], z_bank[piece][:], ACT.Exp, bias=minus_max[piece][:], accum_out=e_sum[piece][:]
                 )
             for piece in range(N_PIECES):
                 inverse_sum = blocks.tile([P, 1], F32, name="inverse_sum")

@@ -10,6 +10,7 @@ PIECE = 512
 SEQS = PIECE // TOKENS
 N_PIECES = LIST // PIECE
 N_HALVES = HIDDEN // P
+N_BANKS = 8
 PIECE_COLS = PIECE // 16
 
 FLOPS = 2 * P * HIDDEN * LIST + 2 * HIDDEN * P * (LIST // TOKENS)
@@ -27,6 +28,7 @@ def tile_heterogeneousgatingnetwork_kernel(tc, table, w1, b1, w2, b2, offs, out)
         tc.tile_pool(name="hidden", bufs=N_PIECES * N_HALVES) as hidden,
         tc.tile_pool(name="work", bufs=3) as work,
         tc.tile_pool(name="blocks", bufs=N_PIECES) as blocks,
+        tc.psum_pool(name="banks", bufs=N_BANKS) as banks,
     ):
         offsets = held.tile([P, LIST // 16], U16, name="offsets")
         nc.sync.dma_start(offsets[:], offs)
@@ -50,55 +52,50 @@ def tile_heterogeneousgatingnetwork_kernel(tc, table, w1, b1, w2, b2, offs, out)
         make_identity(nc, identity[:])
 
         a = [[None] * N_HALVES for piece in range(N_PIECES)]
-        with tc.psum_pool(name="proj_banks", bufs=N_PIECES * N_HALVES) as proj_banks:
-            for piece in range(N_PIECES):
-                piece_offsets = offsets[:, piece * PIECE_COLS : (piece + 1) * PIECE_COLS]
-                for h in range(N_HALVES):
-                    proj = proj_banks.tile([P, PIECE], F32, name="proj")
-                    nc.tensor.matmul(
-                        proj[:],
-                        w1_sb[:, h * P : (h + 1) * P],
-                        table_sb[:].indirect(piece_offsets),
-                        start=True,
-                        stop=True,
-                    )
-                    token_sum = work.tile([P, SEQS], F32, name="token_sum")
-                    nc.vector.tensor_reduce(
-                        token_sum[:], proj[:].rearrange("i (r t) -> i r t", t=TOKENS), axis=X, op=ALU.add
-                    )
-                    a[piece][h] = hidden.tile([P, SEQS], BF16, name="a")
-                    nc.scalar.activation(
-                        a[piece][h][:], token_sum[:], ACT.Gelu, bias=b1_half[h][:], scale=1.0 / TOKENS
-                    )
-
-        with (
-            tc.psum_pool(name="gate_banks", bufs=N_PIECES) as gate_banks,
-            tc.psum_pool(name="flip_banks", bufs=N_PIECES) as flip_banks,
-        ):
-            z_bank, minus_max = [], []
-            for piece in range(N_PIECES):
-                z_bank.append(gate_banks.tile([P, P], F32, name="z_bank"))
-                nc.tensor.matmul(z_bank[piece][:], identity[:], b2_rows[:], start=True, stop=False)
-                for h in range(N_HALVES):
-                    nc.tensor.matmul(
-                        z_bank[piece][:], a[piece][h][:], w2_sb[:, h, :], start=False, stop=(h == N_HALVES - 1)
-                    )
-                minus_max.append(blocks.tile([P, 1], F32, name="minus_max"))
-                nc.vector.tensor_reduce(minus_max[piece][:], z_bank[piece][:], axis=X, op=ALU.max, negate=True)
-            e, e_sum = [], []
-            for piece in range(N_PIECES):
-                e.append(blocks.tile([P, P], F32, name="e"))
-                e_sum.append(blocks.tile([P, 1], F32, name="e_sum"))
-                nc.scalar.activation(
-                    e[piece][:], z_bank[piece][:], ACT.Exp, bias=minus_max[piece][:], accum_out=e_sum[piece][:]
+        for piece in range(N_PIECES):
+            piece_offsets = offsets[:, piece * PIECE_COLS : (piece + 1) * PIECE_COLS]
+            for h in range(N_HALVES):
+                proj = banks.tile([P, PIECE], F32, name="proj", tag="bank")
+                nc.tensor.matmul(
+                    proj[:],
+                    w1_sb[:, h * P : (h + 1) * P],
+                    table_sb[:].indirect(piece_offsets),
+                    start=True,
+                    stop=True,
                 )
-            for piece in range(N_PIECES):
-                inverse_sum = blocks.tile([P, 1], F32, name="inverse_sum")
-                nc.vector.reciprocal(inverse_sum[:], e_sum[piece][:])
-                share = blocks.tile([P, P], F32, name="share")
-                nc.vector.tensor_scalar_mul(share[:], e[piece][:], inverse_sum[:])
-                flipped = flip_banks.tile([P, P], F32, name="flipped")
-                nc.tensor.transpose(flipped[:], share[:], identity[:])
-                out_block = blocks.tile([P, SEQS], F32, name="out_block")
-                nc.scalar.copy(out_block[:], flipped[:])
-                nc.sync.dma_start(out[:, piece * SEQS : (piece + 1) * SEQS], out_block[:])
+                token_sum = work.tile([P, SEQS], F32, name="token_sum")
+                nc.vector.tensor_reduce(
+                    token_sum[:], proj[:].rearrange("i (r t) -> i r t", t=TOKENS), axis=X, op=ALU.add
+                )
+                a[piece][h] = hidden.tile([P, SEQS], BF16, name="a")
+                nc.scalar.activation(
+                    a[piece][h][:], token_sum[:], ACT.Gelu, bias=b1_half[h][:], scale=1.0 / TOKENS
+                )
+
+        z_bank, minus_max = [], []
+        for piece in range(N_PIECES):
+            z_bank.append(banks.tile([P, P], F32, name="z_bank", tag="bank"))
+            nc.tensor.matmul(z_bank[piece][:], identity[:], b2_rows[:], start=True, stop=False)
+            for h in range(N_HALVES):
+                nc.tensor.matmul(
+                    z_bank[piece][:], a[piece][h][:], w2_sb[:, h, :], start=False, stop=(h == N_HALVES - 1)
+                )
+            minus_max.append(blocks.tile([P, 1], F32, name="minus_max"))
+            nc.vector.tensor_reduce(minus_max[piece][:], z_bank[piece][:], axis=X, op=ALU.max, negate=True)
+        e, e_sum = [], []
+        for piece in range(N_PIECES):
+            e.append(blocks.tile([P, P], F32, name="e"))
+            e_sum.append(blocks.tile([P, 1], F32, name="e_sum"))
+            nc.scalar.activation(
+                e[piece][:], z_bank[piece][:], ACT.Exp, bias=minus_max[piece][:], accum_out=e_sum[piece][:]
+            )
+        for piece in range(N_PIECES):
+            inverse_sum = blocks.tile([P, 1], F32, name="inverse_sum")
+            nc.vector.reciprocal(inverse_sum[:], e_sum[piece][:])
+            share = blocks.tile([P, P], F32, name="share")
+            nc.vector.tensor_scalar_mul(share[:], e[piece][:], inverse_sum[:])
+            flipped = banks.tile([P, P], F32, name="flipped", tag="bank")
+            nc.tensor.transpose(flipped[:], share[:], identity[:])
+            out_block = blocks.tile([P, SEQS], F32, name="out_block")
+            nc.scalar.copy(out_block[:], flipped[:])
+            nc.sync.dma_start(out[:, piece * SEQS : (piece + 1) * SEQS], out_block[:])

@@ -1,3 +1,5 @@
+import math
+
 import concourse.mybir as mybir
 from concourse.masks import make_identity
 
@@ -11,6 +13,8 @@ SEQS = PIECE // TOKENS
 N_PIECES = LIST // PIECE
 N_HALVES = HIDDEN // P
 N_BANKS = 8
+SHIFT = 6.0
+SLOPE = math.sqrt(2.0 * math.pi) / 4.0
 PIECE_COLS = PIECE // 16
 
 FLOPS = 2 * P * HIDDEN * LIST + 2 * HIDDEN * P * (LIST // TOKENS)
@@ -46,10 +50,17 @@ def tile_heterogeneousgatingnetwork_kernel(tc, table, w1, b1, w2, b2, offs, out)
         b1_half = [held.tile([P, 1], F32, name=f"b1_half{h}") for h in range(N_HALVES)]
         for h in range(N_HALVES):
             nc.sync.dma_start(b1_half[h][:], b1[h * P : (h + 1) * P, :])
-        b2_rows = held.tile([P, P], F32, name="b2_rows")
-        nc.sync.dma_start(b2_rows[:], b2.rearrange("e o -> (e o)").partition_broadcast(P))
+        b2_column = held.tile([P, 1], F32, name="b2_column")
+        nc.sync.dma_start(b2_column[:], b2)
+        w2_half = held.tile([P, N_HALVES, P], BF16, name="w2_half")
+        nc.gpsimd.tensor_scalar(w2_half[:], w2_sb[:], 0.5, 0.0, ALU.mult, ALU.add)
+        b2_half = held.tile([P, 1], F32, name="b2_half")
+        nc.gpsimd.tensor_scalar(b2_half[:], b2_column[:], 0.5, 0.0, ALU.mult, ALU.add)
         identity = held.tile([P, P], F32, name="identity")
         make_identity(nc, identity[:])
+
+        slope = held.tile([P, 1], F32, name="slope")
+        nc.gpsimd.memset(slope[:], SLOPE)
 
         a = [[None] * N_HALVES for piece in range(N_PIECES)]
         for piece in range(N_PIECES):
@@ -72,28 +83,40 @@ def tile_heterogeneousgatingnetwork_kernel(tc, table, w1, b1, w2, b2, offs, out)
                     a[piece][h][:], token_sum[:], ACT.Gelu, bias=b1_half[h][:], scale=1.0 / TOKENS
                 )
 
-        z_bank, minus_max = [], []
+        half_z, peak = [], []
         for piece in range(N_PIECES):
-            z_bank.append(banks.tile([P, P], F32, name="z_bank", tag="bank"))
-            nc.tensor.matmul(z_bank[piece][:], identity[:], b2_rows[:], start=True, stop=False)
+            half_z.append(banks.tile([P, P], F32, name="half_z", tag="bank"))
+            nc.tensor.matmul(
+                half_z[piece][:],
+                b2_half[:].to_broadcast([P, P]),
+                identity[:],
+                start=True,
+                stop=False,
+                is_transpose=True,
+            )
             for h in range(N_HALVES):
                 nc.tensor.matmul(
-                    z_bank[piece][:], a[piece][h][:], w2_sb[:, h, :], start=False, stop=(h == N_HALVES - 1)
+                    half_z[piece][:], a[piece][h][:], w2_half[:, h, :], start=False, stop=(h == N_HALVES - 1)
                 )
-            minus_max.append(blocks.tile([P, 1], F32, name="minus_max"))
-            nc.vector.tensor_reduce(minus_max[piece][:], z_bank[piece][:], axis=X, op=ALU.max, negate=True)
-        e, e_sum = [], []
-        for piece in range(N_PIECES):
-            e.append(blocks.tile([P, P], F32, name="e"))
-            e_sum.append(blocks.tile([P, 1], F32, name="e_sum"))
-            nc.scalar.activation(
-                e[piece][:], z_bank[piece][:], ACT.Exp, bias=minus_max[piece][:], accum_out=e_sum[piece][:]
+            shifted = blocks.tile([P, P], F32, name="shifted")
+            peak.append(blocks.tile([P, 1], F32, name="peak"))
+            nc.vector.tensor_scalar(
+                shifted[:], half_z[piece][:], SHIFT / 2, None, ALU.add, ALU.max, accum_out=peak[piece][:]
             )
+        e, inverse_sum = [], []
         for piece in range(N_PIECES):
-            inverse_sum = blocks.tile([P, 1], F32, name="inverse_sum")
-            nc.vector.reciprocal(inverse_sum[:], e_sum[piece][:])
+            t = blocks.tile([P, P], F32, name="t")
+            nc.scalar.activation(t[:], half_z[piece][:], ACT.Tanh, bias=peak[piece][:], scale=-1.0)
+            e.append(blocks.tile([P, P], F32, name="e"))
+            e_sum = blocks.tile([P, 1], F32, name="e_sum")
+            nc.scalar.activation(
+                e[piece][:], t[:], ACT.Gelu, bias=slope[:], scale=-SLOPE, accum_out=e_sum[:]
+            )
+            inverse_sum.append(blocks.tile([P, 1], F32, name="inverse_sum"))
+            nc.vector.reciprocal(inverse_sum[piece][:], e_sum[:])
+        for piece in range(N_PIECES):
             share = blocks.tile([P, P], F32, name="share")
-            nc.vector.tensor_scalar_mul(share[:], e[piece][:], inverse_sum[:])
+            nc.vector.tensor_scalar_mul(share[:], e[piece][:], inverse_sum[piece][:])
             flipped = banks.tile([P, P], F32, name="flipped", tag="bank")
             nc.tensor.transpose(flipped[:], share[:], identity[:])
             out_block = blocks.tile([P, SEQS], F32, name="out_block")

@@ -114,7 +114,7 @@ def tile_heterogeneousgatingnetwork_kernel(tc, table, w1, b1, w2, b2, offs, out)
             )
             inverse_sum.append(blocks.tile([P, 1], F32, name="inverse_sum"))
             nc.vector.reciprocal(inverse_sum[piece][:], e_sum[:])
-        for piece in range(N_PIECES):
+        for piece in range(N_PIECES - 1):
             share = blocks.tile([P, P], F32, name="share")
             nc.vector.tensor_scalar_mul(share[:], e[piece][:], inverse_sum[piece][:])
             flipped = banks.tile([P, P], F32, name="flipped", tag="bank")
@@ -122,3 +122,13 @@ def tile_heterogeneousgatingnetwork_kernel(tc, table, w1, b1, w2, b2, offs, out)
             out_block = blocks.tile([P, SEQS], F32, name="out_block")
             nc.scalar.copy(out_block[:], flipped[:])
             nc.sync.dma_start(out[:, piece * SEQS : (piece + 1) * SEQS], out_block[:])
+        last = N_PIECES - 1
+        flipped = banks.tile([P, P], F32, name="flipped", tag="bank")
+        nc.tensor.transpose(flipped[:], e[last][:], identity[:])
+        e_flipped = blocks.tile([P, SEQS], F32, name="e_flipped")
+        nc.scalar.copy(e_flipped[:], flipped[:])
+        inverse_rows = banks.tile([P, SEQS], F32, name="inverse_rows", tag="bank")
+        nc.tensor.transpose(inverse_rows[:], inverse_sum[last][:].to_broadcast([P, P]), identity[:])
+        out_block = blocks.tile([P, SEQS], F32, name="out_block")
+        nc.vector.tensor_tensor(out_block[:], inverse_rows[:], e_flipped[:], ALU.mult)
+        nc.sync.dma_start(out[:, last * SEQS :], out_block[:])

@@ -64,24 +64,31 @@ def tile_heterogeneousgatingnetwork_kernel(tc, table, w1, b1, w2, b2, offs, out)
 
         a = [[None] * N_HALVES for piece in range(N_PIECES)]
         for piece in range(N_PIECES):
-            piece_offsets = offsets[:, piece * PIECE_COLS : (piece + 1) * PIECE_COLS]
             for h in range(N_HALVES):
-                proj = banks.tile([P, PIECE], F32, name="proj", tag="bank")
-                nc.tensor.matmul(
-                    proj[:],
-                    w1_sb[:, h * P : (h + 1) * P],
-                    table_sb[:].indirect(piece_offsets),
-                    start=True,
-                    stop=True,
-                )
-                token_sum = work.tile([P, SEQS], F32, name="token_sum")
-                nc.vector.tensor_reduce(
-                    token_sum[:], proj[:].rearrange("i (r t) -> i r t", t=TOKENS), axis=X, op=ALU.add
-                )
                 a[piece][h] = hidden.tile([P, SEQS], BF16, name="a")
-                nc.scalar.activation(
-                    a[piece][h][:], token_sum[:], ACT.Gelu, bias=b1_half[h][:], scale=1.0 / TOKENS
-                )
+                n_parts = 2 if (piece, h) == (N_PIECES - 1, N_HALVES - 1) else 1
+                cols, seqs = PIECE_COLS // n_parts, SEQS // n_parts
+                for part in range(n_parts):
+                    first_col = piece * PIECE_COLS + part * cols
+                    proj = banks.tile([P, seqs * TOKENS], F32, name="proj", tag="bank")
+                    nc.tensor.matmul(
+                        proj[:],
+                        w1_sb[:, h * P : (h + 1) * P],
+                        table_sb[:].indirect(offsets[:, first_col : first_col + cols]),
+                        start=True,
+                        stop=True,
+                    )
+                    token_sum = work.tile([P, seqs], F32, name="token_sum")
+                    nc.vector.tensor_reduce(
+                        token_sum[:], proj[:].rearrange("i (r t) -> i r t", t=TOKENS), axis=X, op=ALU.add
+                    )
+                    nc.scalar.activation(
+                        a[piece][h][:, part * seqs : (part + 1) * seqs],
+                        token_sum[:],
+                        ACT.Gelu,
+                        bias=b1_half[h][:],
+                        scale=1.0 / TOKENS,
+                    )
 
         half_z, peak = [], []
         for piece in range(N_PIECES):
@@ -103,14 +110,14 @@ def tile_heterogeneousgatingnetwork_kernel(tc, table, w1, b1, w2, b2, offs, out)
             nc.vector.tensor_scalar(
                 shifted[:], half_z[piece][:], SHIFT / 2, None, ALU.add, ALU.max, accum_out=peak[piece][:]
             )
-        e, inverse_sum = [], []
+        t, e, inverse_sum = [], [], []
         for piece in range(N_PIECES):
-            t = blocks.tile([P, P], F32, name="t")
-            nc.scalar.activation(t[:], half_z[piece][:], ACT.Tanh, bias=peak[piece][:], scale=-1.0)
+            t.append(blocks.tile([P, P], F32, name="t"))
+            nc.scalar.activation(t[piece][:], half_z[piece][:], ACT.Tanh, bias=peak[piece][:], scale=-1.0)
             e.append(blocks.tile([P, P], F32, name="e"))
             e_sum = blocks.tile([P, 1], F32, name="e_sum")
             nc.scalar.activation(
-                e[piece][:], t[:], ACT.Gelu, bias=slope[:], scale=-SLOPE, accum_out=e_sum[:]
+                e[piece][:], t[piece][:], ACT.Gelu, bias=slope[:], scale=-SLOPE, accum_out=e_sum[:]
             )
             inverse_sum.append(blocks.tile([P, 1], F32, name="inverse_sum"))
             nc.vector.reciprocal(inverse_sum[piece][:], e_sum[:])
@@ -124,9 +131,9 @@ def tile_heterogeneousgatingnetwork_kernel(tc, table, w1, b1, w2, b2, offs, out)
             nc.sync.dma_start(out[:, piece * SEQS : (piece + 1) * SEQS], out_block[:])
         last = N_PIECES - 1
         flipped = banks.tile([P, P], F32, name="flipped", tag="bank")
-        nc.tensor.transpose(flipped[:], e[last][:], identity[:])
+        nc.tensor.transpose(flipped[:], t[last][:], identity[:])
         e_flipped = blocks.tile([P, SEQS], F32, name="e_flipped")
-        nc.scalar.copy(e_flipped[:], flipped[:])
+        nc.scalar.activation(e_flipped[:], flipped[:], ACT.Gelu, bias=slope[:], scale=-SLOPE)
         inverse_rows = banks.tile([P, SEQS], F32, name="inverse_rows", tag="bank")
         nc.tensor.transpose(inverse_rows[:], inverse_sum[last][:].to_broadcast([P, P]), identity[:])
         out_block = blocks.tile([P, SEQS], F32, name="out_block")

import math

import concourse.mybir as mybir
from concourse.masks import make_identity

P = 128
WORDS = 2048
HIDDEN = 256
TOKENS = 4
LIST = 2048
PIECE = 512
SEQS = PIECE // TOKENS
N_PIECES = LIST // PIECE
N_HALVES = HIDDEN // P
N_BANKS = 8
SHIFT = 6.0
SLOPE = math.sqrt(2.0 * math.pi) / 4.0
PIECE_COLS = PIECE // 16

FLOPS = 2 * P * HIDDEN * LIST + 2 * HIDDEN * P * (LIST // TOKENS)

BF16, F32, U16 = mybir.dt.bfloat16, mybir.dt.float32, mybir.dt.uint16
ACT = mybir.ActivationFunctionType
ALU = mybir.AluOpType
X = mybir.AxisListType.X


def tile_heterogeneousgatingnetwork_kernel(tc, table, w1, b1, w2, b2, offs, out):
    nc = tc.nc
    with (
        tc.tile_pool(name="held", bufs=1) as held,
        tc.tile_pool(name="hidden", bufs=N_PIECES * N_HALVES) as hidden,
        tc.tile_pool(name="work", bufs=3) as work,
        tc.tile_pool(name="blocks", bufs=N_PIECES) as blocks,
        tc.psum_pool(name="banks", bufs=N_BANKS) as banks,
    ):
        offsets = held.tile([P, LIST // 16], U16, name="offsets")
        nc.sync.dma_start(offsets[:], offs)
        w1_sb = held.tile([P, HIDDEN], BF16, name="w1_sb")
        nc.scalar.dma_start(w1_sb[:], w1)
        table_sb = held.tile([P, WORDS], BF16, name="table_sb")
        quarter = WORDS // 4
        for q in range(4):
            queue = nc.sync if q % 2 == 0 else nc.scalar
            queue.dma_start(
                table_sb[:, q * quarter : (q + 1) * quarter], table[:, q * quarter : (q + 1) * quarter]
            )
        w2_sb = held.tile([P, N_HALVES, P], BF16, name="w2_sb")
        nc.scalar.dma_start(w2_sb[:], w2.rearrange("(h i) e -> i h e", i=P))
        b1_half = [held.tile([P, 1], F32, name=f"b1_half{h}") for h in range(N_HALVES)]
        for h in range(N_HALVES):
            nc.sync.dma_start(b1_half[h][:], b1[h * P : (h + 1) * P, :])
        b2_column = held.tile([P, 1], F32, name="b2_column")
        nc.sync.dma_start(b2_column[:], b2)
        w2_half = held.tile([P, N_HALVES, P], BF16, name="w2_half")
        nc.gpsimd.tensor_scalar(w2_half[:], w2_sb[:], 0.5, 0.0, ALU.mult, ALU.add)
        b2_half = held.tile([P, 1], F32, name="b2_half")
        nc.gpsimd.tensor_scalar(b2_half[:], b2_column[:], 0.5, 0.0, ALU.mult, ALU.add)
        identity = held.tile([P, P], F32, name="identity")
        make_identity(nc, identity[:])

        slope = held.tile([P, 1], F32, name="slope")
        nc.gpsimd.memset(slope[:], SLOPE)

        a = [[None] * N_HALVES for piece in range(N_PIECES)]
        for piece in range(N_PIECES):
            for h in range(N_HALVES):
                a[piece][h] = hidden.tile([P, SEQS], BF16, name="a")
                n_parts = 2 if (piece, h) == (N_PIECES - 1, N_HALVES - 1) else 1
                cols, seqs = PIECE_COLS // n_parts, SEQS // n_parts
                for part in range(n_parts):
                    first_col = piece * PIECE_COLS + part * cols
                    proj = banks.tile([P, seqs * TOKENS], F32, name="proj", tag="bank")
                    nc.tensor.matmul(
                        proj[:],
                        w1_sb[:, h * P : (h + 1) * P],
                        table_sb[:].indirect(offsets[:, first_col : first_col + cols]),
                        start=True,
                        stop=True,
                    )
                    token_sum = work.tile([P, seqs], F32, name="token_sum")
                    nc.vector.tensor_reduce(
                        token_sum[:], proj[:].rearrange("i (r t) -> i r t", t=TOKENS), axis=X, op=ALU.add
                    )
                    nc.scalar.activation(
                        a[piece][h][:, part * seqs : (part + 1) * seqs],
                        token_sum[:],
                        ACT.Gelu,
                        bias=b1_half[h][:],
                        scale=1.0 / TOKENS,
                    )

        half_z, peak = [], []
        for piece in range(N_PIECES):
            half_z.append(banks.tile([P, P], F32, name="half_z", tag="bank"))
            nc.tensor.matmul(
                half_z[piece][:],
                b2_half[:].to_broadcast([P, P]),
                identity[:],
                start=True,
                stop=False,
                is_transpose=True,
            )
            for h in range(N_HALVES):
                nc.tensor.matmul(
                    half_z[piece][:], a[piece][h][:], w2_half[:, h, :], start=False, stop=(h == N_HALVES - 1)
                )
            shifted = blocks.tile([P, P], F32, name="shifted")
            peak.append(blocks.tile([P, 1], F32, name="peak"))
            nc.vector.tensor_scalar(
                shifted[:], half_z[piece][:], SHIFT / 2, None, ALU.add, ALU.max, accum_out=peak[piece][:]
            )
        t, e, inverse_sum = [], [], []
        for piece in range(N_PIECES):
            t.append(blocks.tile([P, P], F32, name="t"))
            nc.scalar.activation(t[piece][:], half_z[piece][:], ACT.Tanh, bias=peak[piece][:], scale=-1.0)
            e.append(blocks.tile([P, P], F32, name="e"))
            e_sum = blocks.tile([P, 1], F32, name="e_sum")
            nc.scalar.activation(
                e[piece][:], t[piece][:], ACT.Gelu, bias=slope[:], scale=-SLOPE, accum_out=e_sum[:]
            )
            inverse_sum.append(blocks.tile([P, 1], F32, name="inverse_sum"))
            nc.vector.reciprocal(inverse_sum[piece][:], e_sum[:])
        for piece in range(N_PIECES - 1):
            share = blocks.tile([P, P], F32, name="share")
            nc.vector.tensor_scalar_mul(share[:], e[piece][:], inverse_sum[piece][:])
            flipped = banks.tile([P, P], F32, name="flipped", tag="bank")
            nc.tensor.transpose(flipped[:], share[:], identity[:])
            out_block = blocks.tile([P, SEQS], F32, name="out_block")
            nc.scalar.copy(out_block[:], flipped[:])
            nc.sync.dma_start(out[:, piece * SEQS : (piece + 1) * SEQS], out_block[:])
        last = N_PIECES - 1
        flipped = banks.tile([P, P], F32, name="flipped", tag="bank")
        nc.tensor.transpose(flipped[:], t[last][:], identity[:])
        e_flipped = blocks.tile([P, SEQS], F32, name="e_flipped")
        nc.scalar.activation(e_flipped[:], flipped[:], ACT.Gelu, bias=slope[:], scale=-SLOPE)
        inverse_rows = banks.tile([P, SEQS], F32, name="inverse_rows", tag="bank")
        nc.tensor.transpose(inverse_rows[:], inverse_sum[last][:].to_broadcast([P, P]), identity[:])
        out_block = blocks.tile([P, SEQS], F32, name="out_block")
        nc.vector.tensor_tensor(out_block[:], inverse_rows[:], e_flipped[:], ALU.mult)
        nc.sync.dma_start(out[:, last * SEQS :], out_block[:])
